import numpy as np
import ml_dtypes

BF16 = ml_dtypes.bfloat16


def bf(x):
    return np.asarray(x, np.float32).astype(BF16)


def f32(x):
    return np.asarray(x, np.float32)


def f64(x):
    return np.asarray(x).astype(np.float64)


def striped(idx):
    return np.tile(idx.reshape(-1, 16).T, (8, 1))


C, H, HD, S, N = 512, 4, 128, 2048, 512


def setup_inputs():
    return {"word_emb": f32(0.7 * np.random.standard_normal((C, S))), "pos_emb": f32(0.7 * np.random.standard_normal((C, N))), "bo": f32(0.1 * np.random.standard_normal((C, 1))), "offs": striped(np.random.permutation(np.tile(np.arange(S), 2))[:N])}


def reference(word_emb, pos_emb, bo, offs):
    idx = offs[:16].T.reshape(-1)
    x = f64(word_emb)[:, idx] + f64(pos_emb)
    xh = x.reshape(H, HD, N)
    energy = np.einsum("hdq,hdk->hqk", xh, xh) / np.sqrt(C)
    p = np.exp(energy - energy.max(axis=2, keepdims=True))
    attn = p / p.sum(axis=2, keepdims=True)
    ctx = np.einsum("hdk,hqk->hdq", xh, attn).reshape(C, N)
    return ctx.mean(axis=1, keepdims=True) + f64(bo)

@@ -1,0 +1,91 @@
+import math
+
+import concourse.mybir as mybir
+from concourse.masks import make_identity
+
+F32, BF16, U16 = mybir.dt.float32, mybir.dt.bfloat16, mybir.dt.uint16
+ADD, MULT = mybir.AluOpType.add, mybir.AluOpType.mult
+EXP = mybir.ActivationFunctionType.Exp
+FREE_AXIS = mybir.AxisListType.X
+
+P = 128
+HEADS = 4
+WORDS = 2048
+TOKENS = 512
+BLOCKS = TOKENS // P
+ENERGY_SCALE = 1.0 / math.sqrt(HEADS * P)
+
+FLOPS = 2 * HEADS * P * TOKENS * TOKENS + 2 * HEADS * TOKENS * TOKENS + 2 * HEADS * P * TOKENS
+
+
+def tile_statementencoder_kernel(tc, word_emb, pos_emb, bo, offs, out):
+    nc = tc.nc
+    with (
+        tc.tile_pool(name="held", bufs=1) as held,
+        tc.tile_pool(name="stats", bufs=8) as stats,
+        tc.tile_pool(name="work", bufs=4) as work,
+        tc.psum_pool(name="energies", bufs=5) as energies,
+        tc.psum_pool(name="colsums", bufs=2) as colsums,
+        tc.psum_pool(name="flipped", bufs=1) as flipped,
+    ):
+        offsets = held.tile([P, TOKENS // 16], U16, name="offsets")
+        nc.sync.dma_start(offsets[:], offs)
+        words, positions = [], []
+        for h in range(HEADS):
+            channels = slice(h * P, (h + 1) * P)
+            position = held.tile([P, TOKENS], F32, name=f"position{h}")
+            nc.sync.dma_start(position[:], pos_emb[channels, :])
+            word = held.tile([P, WORDS], F32, name=f"word{h}")
+            nc.sync.dma_start(word[:], word_emb[channels, :])
+            positions.append(position)
+            words.append(word)
+        bias_rows = held.tile([HEADS, P], F32, name="bias_rows")
+        nc.sync.dma_start(bias_rows[:], bo.rearrange("(h d) o -> h (d o)", h=HEADS))
+
+        identity = held.tile([P, P], F32, name="identity")
+        make_identity(nc, identity[:])
+        mean_weights = held.tile([P, P], BF16, name="mean_weights")
+        nc.vector.memset(mean_weights[:], 1.0 / TOKENS)
+
+        pooled = held.tile([P, HEADS], F32, name="pooled")
+
+        for h in range(HEADS):
+            x = held.tile([P, TOKENS], F32, name=f"x{h}")
+            nc.vector.tensor_tensor(x[:], words[h][:].indirect(offsets[:]), positions[h][:], ADD)
+            x_bf16 = held.tile([P, TOKENS], BF16, name=f"x_bf16_{h}")
+            nc.scalar.copy(x_bf16[:], x[:])
+
+            colsum = colsums.tile([P, TOKENS], F32, name="colsum")
+            for b in range(BLOCKS):
+                queries = slice(b * P, (b + 1) * P)
+                energy = energies.tile([P, TOKENS], F32, name="energy")
+                nc.tensor.matmul(energy[:], x_bf16[:, queries], x_bf16[:], start=True, stop=True)
+
+                neg_max = stats.tile([P, 1], F32, name="neg_max")
+                nc.vector.reduce_max(neg_max[:], energy[:], axis=FREE_AXIS, negate=True)
+                shift = stats.tile([P, 1], F32, name="shift")
+                nc.scalar.mul(shift[:], neg_max[:], ENERGY_SCALE)
+                expd = work.tile([P, TOKENS], F32, name="expd")
+                row_sum = stats.tile([P, 1], F32, name="row_sum")
+                nc.scalar.activation(
+                    expd[:], energy[:], EXP, bias=shift[:], scale=ENERGY_SCALE, accum_out=row_sum[:]
+                )
+                inv_sum = stats.tile([P, 1], F32, name="inv_sum")
+                nc.vector.reciprocal(inv_sum[:], row_sum[:])
+                attn = work.tile([P, TOKENS], BF16, name="attn")
+                nc.gpsimd.tensor_scalar_mul(attn[:], expd[:], inv_sum[:])
+
+                nc.tensor.matmul(
+                    colsum[:], mean_weights[:], attn[:], start=(b == 0), stop=(b == BLOCKS - 1)
+                )
+
+            weighted = work.tile([P, TOKENS], F32, name="weighted")
+            nc.vector.scalar_tensor_tensor(
+                weighted[:], colsum[:], 1.0, x[:], MULT, MULT, accum_out=pooled[:, h : h + 1]
+            )
+
+        pooled_rows = flipped.tile([HEADS, P], F32, name="pooled_rows")
+        nc.tensor.transpose(pooled_rows[:], pooled[:], identity[:])
+        out_rows = held.tile([HEADS, P], F32, name="out_rows")
+        nc.vector.tensor_tensor(out_rows[:], pooled_rows[:], bias_rows[:], ADD)
+        nc.sync.dma_start(out.rearrange("(h d) o -> h (d o)", h=HEADS), out_rows[:])

@@ -5,7 +5,7 @@ from concourse.masks import make_identity
 
 F32, BF16, U16 = mybir.dt.float32, mybir.dt.bfloat16, mybir.dt.uint16
 ADD, MULT = mybir.AluOpType.add, mybir.AluOpType.mult
-EXP = mybir.ActivationFunctionType.Exp
+EXP, COPY = mybir.ActivationFunctionType.Exp, mybir.ActivationFunctionType.Copy
 FREE_AXIS = mybir.AxisListType.X
 
 P = 128
@@ -49,40 +49,63 @@ def tile_statementencoder_kernel(tc, word_emb, pos_emb, bo, offs, out):
 
         pooled = held.tile([P, HEADS], F32, name="pooled")
 
-        for h in range(HEADS):
-            x = held.tile([P, TOKENS], F32, name=f"x{h}")
-            nc.vector.tensor_tensor(x[:], words[h][:].indirect(offsets[:]), positions[h][:], ADD)
-            x_bf16 = held.tile([P, TOKENS], BF16, name=f"x_bf16_{h}")
-            nc.scalar.copy(x_bf16[:], x[:])
+        x, x_bf16, colsum, expd, row_sum = {}, {}, {}, {}, {}
 
-            colsum = colsums.tile([P, TOKENS], F32, name="colsum")
-            for b in range(BLOCKS):
-                queries = slice(b * P, (b + 1) * P)
-                energy = energies.tile([P, TOKENS], F32, name="energy")
-                nc.tensor.matmul(energy[:], x_bf16[:, queries], x_bf16[:], start=True, stop=True)
+        def embed(h):
+            x[h] = held.tile([P, TOKENS], F32, name=f"x{h}")
+            nc.vector.tensor_tensor(x[h][:], words[h][:].indirect(offsets[:]), positions[h][:], ADD)
+            x_bf16[h] = held.tile([P, TOKENS], BF16, name=f"x_bf16_{h}")
+            nc.scalar.copy(x_bf16[h][:], x[h][:])
 
-                neg_max = stats.tile([P, 1], F32, name="neg_max")
-                nc.vector.reduce_max(neg_max[:], energy[:], axis=FREE_AXIS, negate=True)
-                shift = stats.tile([P, 1], F32, name="shift")
-                nc.scalar.mul(shift[:], neg_max[:], ENERGY_SCALE)
-                expd = work.tile([P, TOKENS], F32, name="expd")
-                row_sum = stats.tile([P, 1], F32, name="row_sum")
-                nc.scalar.activation(
-                    expd[:], energy[:], EXP, bias=shift[:], scale=ENERGY_SCALE, accum_out=row_sum[:]
-                )
-                inv_sum = stats.tile([P, 1], F32, name="inv_sum")
-                nc.vector.reciprocal(inv_sum[:], row_sum[:])
-                attn = work.tile([P, TOKENS], BF16, name="attn")
-                nc.gpsimd.tensor_scalar_mul(attn[:], expd[:], inv_sum[:])
+        def exponentials(h, b):
+            energy = energies.tile([P, TOKENS], F32, name="energy")
+            nc.tensor.matmul(
+                energy[:], x_bf16[h][:, b * P : (b + 1) * P], x_bf16[h][:], start=True, stop=True
+            )
+            neg_max = stats.tile([P, 1], F32, name="neg_max")
+            nc.vector.reduce_max(neg_max[:], energy[:], axis=FREE_AXIS, negate=True)
+            shift = stats.tile([P, 1], F32, name="shift")
+            nc.scalar.mul(shift[:], neg_max[:], ENERGY_SCALE)
+            expd[h, b] = work.tile([P, TOKENS], F32, name="expd")
+            row_sum[h, b] = stats.tile([P, 1], F32, name="row_sum")
+            nc.scalar.activation(
+                expd[h, b][:], energy[:], EXP, bias=shift[:], scale=ENERGY_SCALE,
+                accum_out=row_sum[h, b][:],
+            )
 
-                nc.tensor.matmul(
-                    colsum[:], mean_weights[:], attn[:], start=(b == 0), stop=(b == BLOCKS - 1)
-                )
+        def normalise(h, b):
+            inv_sum = stats.tile([P, 1], F32, name="inv_sum")
+            nc.vector.reciprocal(inv_sum[:], row_sum[h, b][:])
+            attn = work.tile([P, TOKENS], BF16, name="attn")
+            if b % 2 == 1:
+                nc.vector.tensor_scalar_mul(attn[:], expd[h, b][:], inv_sum[:])
+            else:
+                nc.scalar.activation(attn[:], expd[h, b][:], COPY, scale=inv_sum[:])
+            if b == 0:
+                colsum[h] = colsums.tile([P, TOKENS], F32, name="colsum")
+            nc.tensor.matmul(
+                colsum[h][:], mean_weights[:], attn[:], start=(b == 0), stop=(b == BLOCKS - 1)
+            )
 
+        def pool_head(h):
             weighted = work.tile([P, TOKENS], F32, name="weighted")
             nc.vector.scalar_tensor_tensor(
-                weighted[:], colsum[:], 1.0, x[:], MULT, MULT, accum_out=pooled[:, h : h + 1]
+                weighted[:], colsum[h][:], 1.0, x[h][:], MULT, MULT, accum_out=pooled[:, h : h + 1]
             )
+
+        NORMALISE_LAG, POOL_LAG = 2, 3
+        pairs = [(h, b) for h in range(HEADS) for b in range(BLOCKS)]
+        embed(0)
+        for step in range(len(pairs) + POOL_LAG):
+            if step < len(pairs):
+                h, b = pairs[step]
+                if b == BLOCKS // 2 and h + 1 < HEADS:
+                    embed(h + 1)
+                exponentials(h, b)
+            if 0 <= step - NORMALISE_LAG < len(pairs):
+                normalise(*pairs[step - NORMALISE_LAG])
+            if step >= POOL_LAG and pairs[step - POOL_LAG][1] == BLOCKS - 1:
+                pool_head(pairs[step - POOL_LAG][0])
 
         pooled_rows = flipped.tile([HEADS, P], F32, name="pooled_rows")
         nc.tensor.transpose(pooled_rows[:], pooled[:], identity[:])

@@ -23,7 +23,7 @@ def tile_statementencoder_kernel(tc, word_emb, pos_emb, bo, offs, out):
     with (
         tc.tile_pool(name="held", bufs=1) as held,
         tc.tile_pool(name="stats", bufs=8) as stats,
-        tc.tile_pool(name="work", bufs=4) as work,
+        tc.tile_pool(name="work", bufs=6) as work,
         tc.psum_pool(name="energies", bufs=5) as energies,
         tc.psum_pool(name="colsums", bufs=2) as colsums,
         tc.psum_pool(name="flipped", bufs=1) as flipped,
@@ -77,7 +77,11 @@ def tile_statementencoder_kernel(tc, word_emb, pos_emb, bo, offs, out):
             inv_sum = stats.tile([P, 1], F32, name="inv_sum")
             nc.vector.reciprocal(inv_sum[:], row_sum[h, b][:])
             attn = work.tile([P, TOKENS], BF16, name="attn")
-            if b % 2 == 1:
+            if b % 2 == 0:
+                nc.gpsimd.tensor_tensor(
+                    attn[:], expd[h, b][:], inv_sum[:].to_broadcast([P, TOKENS]), MULT
+                )
+            elif b == BLOCKS - 1:
                 nc.vector.tensor_scalar_mul(attn[:], expd[h, b][:], inv_sum[:])
             else:
                 nc.scalar.activation(attn[:], expd[h, b][:], COPY, scale=inv_sum[:])

@@ -23,7 +23,7 @@ def tile_statementencoder_kernel(tc, word_emb, pos_emb, bo, offs, out):
     with (
         tc.tile_pool(name="held", bufs=1) as held,
         tc.tile_pool(name="stats", bufs=8) as stats,
-        tc.tile_pool(name="work", bufs=6) as work,
+        tc.tile_pool(name="work", bufs=4) as work,
         tc.psum_pool(name="energies", bufs=5) as energies,
         tc.psum_pool(name="colsums", bufs=2) as colsums,
         tc.psum_pool(name="flipped", bufs=1) as flipped,
@@ -49,67 +49,43 @@ def tile_statementencoder_kernel(tc, word_emb, pos_emb, bo, offs, out):
 
         pooled = held.tile([P, HEADS], F32, name="pooled")
 
-        x, x_bf16, colsum, expd, row_sum = {}, {}, {}, {}, {}
+        for h in range(HEADS):
+            x = held.tile([P, TOKENS], F32, name=f"x{h}")
+            nc.vector.tensor_tensor(x[:], words[h][:].indirect(offsets[:]), positions[h][:], ADD)
+            x_bf16 = held.tile([P, TOKENS], BF16, name=f"x_bf16_{h}")
+            nc.scalar.copy(x_bf16[:], x[:])
 
-        def embed(h):
-            x[h] = held.tile([P, TOKENS], F32, name=f"x{h}")
-            nc.vector.tensor_tensor(x[h][:], words[h][:].indirect(offsets[:]), positions[h][:], ADD)
-            x_bf16[h] = held.tile([P, TOKENS], BF16, name=f"x_bf16_{h}")
-            nc.scalar.copy(x_bf16[h][:], x[h][:])
+            colsum = colsums.tile([P, TOKENS], F32, name="colsum")
+            for b in range(BLOCKS):
+                queries = slice(b * P, (b + 1) * P)
+                energy = energies.tile([P, TOKENS], F32, name="energy")
+                nc.tensor.matmul(energy[:], x_bf16[:, queries], x_bf16[:], start=True, stop=True)
 
-        def exponentials(h, b):
-            energy = energies.tile([P, TOKENS], F32, name="energy")
-            nc.tensor.matmul(
-                energy[:], x_bf16[h][:, b * P : (b + 1) * P], x_bf16[h][:], start=True, stop=True
-            )
-            neg_max = stats.tile([P, 1], F32, name="neg_max")
-            nc.vector.reduce_max(neg_max[:], energy[:], axis=FREE_AXIS, negate=True)
-            shift = stats.tile([P, 1], F32, name="shift")
-            nc.scalar.mul(shift[:], neg_max[:], ENERGY_SCALE)
-            expd[h, b] = work.tile([P, TOKENS], F32, name="expd")
-            row_sum[h, b] = stats.tile([P, 1], F32, name="row_sum")
-            nc.scalar.activation(
-                expd[h, b][:], energy[:], EXP, bias=shift[:], scale=ENERGY_SCALE,
-                accum_out=row_sum[h, b][:],
-            )
-
-        def normalise(h, b):
-            inv_sum = stats.tile([P, 1], F32, name="inv_sum")
-            nc.vector.reciprocal(inv_sum[:], row_sum[h, b][:])
-            attn = work.tile([P, TOKENS], BF16, name="attn")
-            if b % 2 == 0:
-                nc.gpsimd.tensor_tensor(
-                    attn[:], expd[h, b][:], inv_sum[:].to_broadcast([P, TOKENS]), MULT
+                neg_max = stats.tile([P, 1], F32, name="neg_max")
+                nc.vector.reduce_max(neg_max[:], energy[:], axis=FREE_AXIS, negate=True)
+                shift = stats.tile([P, 1], F32, name="shift")
+                nc.scalar.mul(shift[:], neg_max[:], ENERGY_SCALE)
+                expd = work.tile([P, TOKENS], F32, name="expd")
+                row_sum = stats.tile([P, 1], F32, name="row_sum")
+                nc.scalar.activation(
+                    expd[:], energy[:], EXP, bias=shift[:], scale=ENERGY_SCALE, accum_out=row_sum[:]
                 )
-            elif b == BLOCKS - 1:
-                nc.vector.tensor_scalar_mul(attn[:], expd[h, b][:], inv_sum[:])
-            else:
-                nc.scalar.activation(attn[:], expd[h, b][:], COPY, scale=inv_sum[:])
-            if b == 0:
-                colsum[h] = colsums.tile([P, TOKENS], F32, name="colsum")
-            nc.tensor.matmul(
-                colsum[h][:], mean_weights[:], attn[:], start=(b == 0), stop=(b == BLOCKS - 1)
-            )
+                inv_sum = stats.tile([P, 1], F32, name="inv_sum")
+                nc.vector.reciprocal(inv_sum[:], row_sum[:])
+                attn = work.tile([P, TOKENS], BF16, name="attn")
+                if b % 2 == 1:
+                    nc.vector.tensor_scalar_mul(attn[:], expd[:], inv_sum[:])
+                else:
+                    nc.scalar.activation(attn[:], expd[:], COPY, scale=inv_sum[:])
 
-        def pool_head(h):
+                nc.tensor.matmul(
+                    colsum[:], mean_weights[:], attn[:], start=(b == 0), stop=(b == BLOCKS - 1)
+                )
+
             weighted = work.tile([P, TOKENS], F32, name="weighted")
             nc.vector.scalar_tensor_tensor(
-                weighted[:], colsum[h][:], 1.0, x[h][:], MULT, MULT, accum_out=pooled[:, h : h + 1]
+                weighted[:], colsum[:], 1.0, x[:], MULT, MULT, accum_out=pooled[:, h : h + 1]
             )
-
-        NORMALISE_LAG, POOL_LAG = 2, 3
-        pairs = [(h, b) for h in range(HEADS) for b in range(BLOCKS)]
-        embed(0)
-        for step in range(len(pairs) + POOL_LAG):
-            if step < len(pairs):
-                h, b = pairs[step]
-                if b == BLOCKS // 2 and h + 1 < HEADS:
-                    embed(h + 1)
-                exponentials(h, b)
-            if 0 <= step - NORMALISE_LAG < len(pairs):
-                normalise(*pairs[step - NORMALISE_LAG])
-            if step >= POOL_LAG and pairs[step - POOL_LAG][1] == BLOCKS - 1:
-                pool_head(pairs[step - POOL_LAG][0])
 
         pooled_rows = flipped.tile([HEADS, P], F32, name="pooled_rows")
         nc.tensor.transpose(pooled_rows[:], pooled[:], identity[:])

@@ -22,8 +22,8 @@ def tile_statementencoder_kernel(tc, word_emb, pos_emb, bo, offs, out):
     nc = tc.nc
     with (
         tc.tile_pool(name="held", bufs=1) as held,
-        tc.tile_pool(name="stats", bufs=8) as stats,
-        tc.tile_pool(name="work", bufs=4) as work,
+        tc.tile_pool(name="stats", bufs=10) as stats,
+        tc.tile_pool(name="work", bufs=6) as work,
         tc.psum_pool(name="energies", bufs=5) as energies,
         tc.psum_pool(name="colsums", bufs=2) as colsums,
         tc.psum_pool(name="flipped", bufs=1) as flipped,
@@ -49,43 +49,67 @@ def tile_statementencoder_kernel(tc, word_emb, pos_emb, bo, offs, out):
 
         pooled = held.tile([P, HEADS], F32, name="pooled")
 
-        for h in range(HEADS):
-            x = held.tile([P, TOKENS], F32, name=f"x{h}")
-            nc.vector.tensor_tensor(x[:], words[h][:].indirect(offsets[:]), positions[h][:], ADD)
-            x_bf16 = held.tile([P, TOKENS], BF16, name=f"x_bf16_{h}")
-            nc.scalar.copy(x_bf16[:], x[:])
+        x, x_bf16, colsum, expd, row_sum, inv_sum = {}, {}, {}, {}, {}, {}
 
-            colsum = colsums.tile([P, TOKENS], F32, name="colsum")
-            for b in range(BLOCKS):
-                queries = slice(b * P, (b + 1) * P)
-                energy = energies.tile([P, TOKENS], F32, name="energy")
-                nc.tensor.matmul(energy[:], x_bf16[:, queries], x_bf16[:], start=True, stop=True)
+        def embed(h):
+            x[h] = held.tile([P, TOKENS], F32, name=f"x{h}")
+            nc.vector.tensor_tensor(x[h][:], words[h][:].indirect(offsets[:]), positions[h][:], ADD)
+            x_bf16[h] = held.tile([P, TOKENS], BF16, name=f"x_bf16_{h}")
+            nc.gpsimd.tensor_copy(x_bf16[h][:], x[h][:])
 
-                neg_max = stats.tile([P, 1], F32, name="neg_max")
-                nc.vector.reduce_max(neg_max[:], energy[:], axis=FREE_AXIS, negate=True)
-                shift = stats.tile([P, 1], F32, name="shift")
-                nc.scalar.mul(shift[:], neg_max[:], ENERGY_SCALE)
-                expd = work.tile([P, TOKENS], F32, name="expd")
-                row_sum = stats.tile([P, 1], F32, name="row_sum")
-                nc.scalar.activation(
-                    expd[:], energy[:], EXP, bias=shift[:], scale=ENERGY_SCALE, accum_out=row_sum[:]
-                )
-                inv_sum = stats.tile([P, 1], F32, name="inv_sum")
-                nc.vector.reciprocal(inv_sum[:], row_sum[:])
-                attn = work.tile([P, TOKENS], BF16, name="attn")
-                if b % 2 == 1:
-                    nc.vector.tensor_scalar_mul(attn[:], expd[:], inv_sum[:])
-                else:
-                    nc.scalar.activation(attn[:], expd[:], COPY, scale=inv_sum[:])
+        def exponentials(h, b):
+            energy = energies.tile([P, TOKENS], F32, name="energy")
+            nc.tensor.matmul(
+                energy[:], x_bf16[h][:, b * P : (b + 1) * P], x_bf16[h][:], start=True, stop=True
+            )
+            neg_max = stats.tile([P, 1], F32, name="neg_max")
+            nc.vector.reduce_max(neg_max[:], energy[:], axis=FREE_AXIS, negate=True)
+            shift = stats.tile([P, 1], F32, name="shift")
+            nc.gpsimd.tensor_scalar_mul(shift[:], neg_max[:], ENERGY_SCALE)
+            expd[h, b] = work.tile([P, TOKENS], F32, name="expd")
+            row_sum[h, b] = stats.tile([P, 1], F32, name="row_sum")
+            nc.scalar.activation(
+                expd[h, b][:], energy[:], EXP, bias=shift[:], scale=ENERGY_SCALE,
+                accum_out=row_sum[h, b][:],
+            )
 
-                nc.tensor.matmul(
-                    colsum[:], mean_weights[:], attn[:], start=(b == 0), stop=(b == BLOCKS - 1)
-                )
+        def invert(h, b):
+            inv_sum[h, b] = stats.tile([P, 1], F32, name="inv_sum")
+            nc.vector.reciprocal(inv_sum[h, b][:], row_sum[h, b][:])
 
+        def normalise(h, b):
+            attn = work.tile([P, TOKENS], BF16, name="attn")
+            if b % 2 == 1:
+                nc.vector.tensor_scalar_mul(attn[:], expd[h, b][:], inv_sum[h, b][:])
+            else:
+                nc.scalar.activation(attn[:], expd[h, b][:], COPY, scale=inv_sum[h, b][:])
+            if b == 0:
+                colsum[h] = colsums.tile([P, TOKENS], F32, name="colsum")
+            nc.tensor.matmul(
+                colsum[h][:], mean_weights[:], attn[:], start=(b == 0), stop=(b == BLOCKS - 1)
+            )
+
+        def pool_head(h):
             weighted = work.tile([P, TOKENS], F32, name="weighted")
             nc.vector.scalar_tensor_tensor(
-                weighted[:], colsum[:], 1.0, x[:], MULT, MULT, accum_out=pooled[:, h : h + 1]
+                weighted[:], colsum[h][:], 1.0, x[h][:], MULT, MULT, accum_out=pooled[:, h : h + 1]
             )
+
+        INVERT_LAG, NORMALISE_LAG, POOL_LAG = 2, 3, 5
+        pairs = [(h, b) for h in range(HEADS) for b in range(BLOCKS)]
+        embed(0)
+        for step in range(len(pairs) + POOL_LAG):
+            if step < len(pairs):
+                h, b = pairs[step]
+                if b == 1 and h + 1 < HEADS:
+                    embed(h + 1)
+                exponentials(h, b)
+            if 0 <= step - INVERT_LAG < len(pairs):
+                invert(*pairs[step - INVERT_LAG])
+            if 0 <= step - NORMALISE_LAG < len(pairs):
+                normalise(*pairs[step - NORMALISE_LAG])
+            if step >= POOL_LAG and pairs[step - POOL_LAG][1] == BLOCKS - 1:
+                pool_head(pairs[step - POOL_LAG][0])
 
         pooled_rows = flipped.tile([HEADS, P], F32, name="pooled_rows")
         nc.tensor.transpose(pooled_rows[:], pooled[:], identity[:])

@@ -5,7 +5,7 @@ from concourse.masks import make_identity
 
 F32, BF16, U16 = mybir.dt.float32, mybir.dt.bfloat16, mybir.dt.uint16
 ADD, MULT = mybir.AluOpType.add, mybir.AluOpType.mult
-EXP, COPY = mybir.ActivationFunctionType.Exp, mybir.ActivationFunctionType.Copy
+EXP = mybir.ActivationFunctionType.Exp
 FREE_AXIS = mybir.AxisListType.X
 
 P = 128
@@ -44,8 +44,6 @@ def tile_statementencoder_kernel(tc, word_emb, pos_emb, bo, offs, out):
 
         identity = held.tile([P, P], F32, name="identity")
         make_identity(nc, identity[:])
-        mean_weights = held.tile([P, P], BF16, name="mean_weights")
-        nc.vector.memset(mean_weights[:], 1.0 / TOKENS)
 
         pooled = held.tile([P, HEADS], F32, name="pooled")
 
@@ -66,7 +64,7 @@ def tile_statementencoder_kernel(tc, word_emb, pos_emb, bo, offs, out):
             nc.vector.reduce_max(neg_max[:], energy[:], axis=FREE_AXIS, negate=True)
             shift = stats.tile([P, 1], F32, name="shift")
             nc.gpsimd.tensor_scalar_mul(shift[:], neg_max[:], ENERGY_SCALE)
-            expd[h, b] = work.tile([P, TOKENS], F32, name="expd")
+            expd[h, b] = work.tile([P, TOKENS], BF16, name="expd")
             row_sum[h, b] = stats.tile([P, 1], F32, name="row_sum")
             nc.scalar.activation(
                 expd[h, b][:], energy[:], EXP, bias=shift[:], scale=ENERGY_SCALE,
@@ -74,19 +72,16 @@ def tile_statementencoder_kernel(tc, word_emb, pos_emb, bo, offs, out):
             )
 
         def invert(h, b):
-            inv_sum[h, b] = stats.tile([P, 1], F32, name="inv_sum")
-            nc.vector.reciprocal(inv_sum[h, b][:], row_sum[h, b][:])
+            inv_sum[h, b] = stats.tile([P, 1], BF16, name="inv_sum")
+            with nc.allow_low_precision(reason="1 / sum is a matmul operand: bfloat16"):
+                nc.vector.reciprocal(inv_sum[h, b][:], row_sum[h, b][:])
 
-        def normalise(h, b):
-            attn = work.tile([P, TOKENS], BF16, name="attn")
-            if b % 2 == 1:
-                nc.vector.tensor_scalar_mul(attn[:], expd[h, b][:], inv_sum[h, b][:])
-            else:
-                nc.scalar.activation(attn[:], expd[h, b][:], COPY, scale=inv_sum[h, b][:])
+        def add_to_colsum(h, b):
             if b == 0:
                 colsum[h] = colsums.tile([P, TOKENS], F32, name="colsum")
             nc.tensor.matmul(
-                colsum[h][:], mean_weights[:], attn[:], start=(b == 0), stop=(b == BLOCKS - 1)
+                colsum[h][:], inv_sum[h, b][:, 0:1].to_broadcast([P, P]), expd[h, b][:],
+                start=(b == 0), stop=(b == BLOCKS - 1),
             )
 
         def pool_head(h):
@@ -95,7 +90,7 @@ def tile_statementencoder_kernel(tc, word_emb, pos_emb, bo, offs, out):
                 weighted[:], colsum[h][:], 1.0, x[h][:], MULT, MULT, accum_out=pooled[:, h : h + 1]
             )
 
-        INVERT_LAG, NORMALISE_LAG, POOL_LAG = 2, 3, 5
+        INVERT_LAG, COLSUM_LAG, POOL_LAG = 2, 3, 5
         pairs = [(h, b) for h in range(HEADS) for b in range(BLOCKS)]
         embed(0)
         for step in range(len(pairs) + POOL_LAG):
@@ -106,13 +101,15 @@ def tile_statementencoder_kernel(tc, word_emb, pos_emb, bo, offs, out):
                 exponentials(h, b)
             if 0 <= step - INVERT_LAG < len(pairs):
                 invert(*pairs[step - INVERT_LAG])
-            if 0 <= step - NORMALISE_LAG < len(pairs):
-                normalise(*pairs[step - NORMALISE_LAG])
+            if 0 <= step - COLSUM_LAG < len(pairs):
+                add_to_colsum(*pairs[step - COLSUM_LAG])
             if step >= POOL_LAG and pairs[step - POOL_LAG][1] == BLOCKS - 1:
                 pool_head(pairs[step - POOL_LAG][0])
 
         pooled_rows = flipped.tile([HEADS, P], F32, name="pooled_rows")
         nc.tensor.transpose(pooled_rows[:], pooled[:], identity[:])
         out_rows = held.tile([HEADS, P], F32, name="out_rows")
-        nc.vector.tensor_tensor(out_rows[:], pooled_rows[:], bias_rows[:], ADD)
+        nc.vector.scalar_tensor_tensor(
+            out_rows[:], pooled_rows[:], 1.0 / TOKENS, bias_rows[:], MULT, ADD
+        )
         nc.sync.dma_start(out.rearrange("(h d) o -> h (d o)", h=HEADS), out_rows[:])

@@ -25,8 +25,7 @@ def tile_statementencoder_kernel(tc, word_emb, pos_emb, bo, offs, out):
         tc.tile_pool(name="stats", bufs=10) as stats,
         tc.tile_pool(name="work", bufs=6) as work,
         tc.psum_pool(name="energies", bufs=5) as energies,
-        tc.psum_pool(name="colsums", bufs=2) as colsums,
-        tc.psum_pool(name="flipped", bufs=1) as flipped,
+        tc.psum_pool(name="colsums", bufs=3) as colsums,
     ):
         offsets = held.tile([P, TOKENS // 16], U16, name="offsets")
         nc.sync.dma_start(offsets[:], offs)
@@ -47,27 +46,30 @@ def tile_statementencoder_kernel(tc, word_emb, pos_emb, bo, offs, out):
 
         pooled = held.tile([P, HEADS], F32, name="pooled")
 
-        x, x_bf16, colsum, expd, row_sum, inv_sum = {}, {}, {}, {}, {}, {}
+        x, x_bf16, energy, colsum, expd, row_sum, inv_sum = {}, {}, {}, {}, {}, {}, {}
 
         def embed(h):
             x[h] = held.tile([P, TOKENS], F32, name=f"x{h}")
             nc.vector.tensor_tensor(x[h][:], words[h][:].indirect(offsets[:]), positions[h][:], ADD)
             x_bf16[h] = held.tile([P, TOKENS], BF16, name=f"x_bf16_{h}")
-            nc.gpsimd.tensor_copy(x_bf16[h][:], x[h][:])
+            nc.scalar.copy(x_bf16[h][:], x[h][:])
+
+        def energies_of(h, b):
+            energy[h, b] = energies.tile([P, TOKENS], F32, name="energy")
+            nc.tensor.matmul(
+                energy[h, b][:], x_bf16[h][:, b * P : (b + 1) * P], x_bf16[h][:],
+                start=True, stop=True,
+            )
 
         def exponentials(h, b):
-            energy = energies.tile([P, TOKENS], F32, name="energy")
-            nc.tensor.matmul(
-                energy[:], x_bf16[h][:, b * P : (b + 1) * P], x_bf16[h][:], start=True, stop=True
-            )
             neg_max = stats.tile([P, 1], F32, name="neg_max")
-            nc.vector.reduce_max(neg_max[:], energy[:], axis=FREE_AXIS, negate=True)
+            nc.vector.reduce_max(neg_max[:], energy[h, b][:], axis=FREE_AXIS, negate=True)
             shift = stats.tile([P, 1], F32, name="shift")
             nc.gpsimd.tensor_scalar_mul(shift[:], neg_max[:], ENERGY_SCALE)
             expd[h, b] = work.tile([P, TOKENS], BF16, name="expd")
             row_sum[h, b] = stats.tile([P, 1], F32, name="row_sum")
             nc.scalar.activation(
-                expd[h, b][:], energy[:], EXP, bias=shift[:], scale=ENERGY_SCALE,
+                expd[h, b][:], energy[h, b][:], EXP, bias=shift[:], scale=ENERGY_SCALE,
                 accum_out=row_sum[h, b][:],
             )
 
@@ -90,11 +92,13 @@ def tile_statementencoder_kernel(tc, word_emb, pos_emb, bo, offs, out):
                 weighted[:], colsum[h][:], 1.0, x[h][:], MULT, MULT, accum_out=pooled[:, h : h + 1]
             )
 
-        INVERT_LAG, COLSUM_LAG, POOL_LAG = 2, 3, 5
+        ENERGY_LEAD, INVERT_LAG, COLSUM_LAG = 2, 2, 3
         pairs = [(h, b) for h in range(HEADS) for b in range(BLOCKS)]
         embed(0)
-        for step in range(len(pairs) + POOL_LAG):
-            if step < len(pairs):
+        for step in range(-ENERGY_LEAD, len(pairs) + COLSUM_LAG):
+            if step + ENERGY_LEAD < len(pairs):
+                energies_of(*pairs[step + ENERGY_LEAD])
+            if 0 <= step < len(pairs):
                 h, b = pairs[step]
                 if b == 1 and h + 1 < HEADS:
                     embed(h + 1)
@@ -103,10 +107,10 @@ def tile_statementencoder_kernel(tc, word_emb, pos_emb, bo, offs, out):
                 invert(*pairs[step - INVERT_LAG])
             if 0 <= step - COLSUM_LAG < len(pairs):
                 add_to_colsum(*pairs[step - COLSUM_LAG])
-            if step >= POOL_LAG and pairs[step - POOL_LAG][1] == BLOCKS - 1:
-                pool_head(pairs[step - POOL_LAG][0])
+        for h in range(HEADS):
+            pool_head(h)
 
-        pooled_rows = flipped.tile([HEADS, P], F32, name="pooled_rows")
+        pooled_rows = energies.tile([HEADS, P], F32, name="pooled_rows", tag="energy")
         nc.tensor.transpose(pooled_rows[:], pooled[:], identity[:])
         out_rows = held.tile([HEADS, P], F32, name="out_rows")
         nc.vector.scalar_tensor_tensor(

@@ -1,5 +1,3 @@
-import math
-
 import concourse.mybir as mybir
 from concourse.masks import make_identity
 
@@ -13,7 +11,7 @@ HEADS = 4
 WORDS = 2048
 TOKENS = 512
 BLOCKS = TOKENS // P
-ENERGY_SCALE = 1.0 / math.sqrt(HEADS * P)
+X_SCALE = (HEADS * P) ** -0.25
 
 FLOPS = 2 * HEADS * P * TOKENS * TOKENS + 2 * HEADS * TOKENS * TOKENS + 2 * HEADS * P * TOKENS
 
@@ -52,7 +50,7 @@ def tile_statementencoder_kernel(tc, word_emb, pos_emb, bo, offs, out):
             x[h] = held.tile([P, TOKENS], F32, name=f"x{h}")
             nc.vector.tensor_tensor(x[h][:], words[h][:].indirect(offsets[:]), positions[h][:], ADD)
             x_bf16[h] = held.tile([P, TOKENS], BF16, name=f"x_bf16_{h}")
-            nc.scalar.copy(x_bf16[h][:], x[h][:])
+            nc.gpsimd.tensor_scalar(x_bf16[h][:], x[h][:], X_SCALE, 0.0, MULT, ADD)
 
         def energies_of(h, b):
             energy[h, b] = energies.tile([P, TOKENS], F32, name="energy")
@@ -64,12 +62,10 @@ def tile_statementencoder_kernel(tc, word_emb, pos_emb, bo, offs, out):
         def exponentials(h, b):
             neg_max = stats.tile([P, 1], F32, name="neg_max")
             nc.vector.reduce_max(neg_max[:], energy[h, b][:], axis=FREE_AXIS, negate=True)
-            shift = stats.tile([P, 1], F32, name="shift")
-            nc.gpsimd.tensor_scalar_mul(shift[:], neg_max[:], ENERGY_SCALE)
             expd[h, b] = work.tile([P, TOKENS], BF16, name="expd")
             row_sum[h, b] = stats.tile([P, 1], F32, name="row_sum")
             nc.scalar.activation(
-                expd[h, b][:], energy[h, b][:], EXP, bias=shift[:], scale=ENERGY_SCALE,
+                expd[h, b][:], energy[h, b][:], EXP, bias=neg_max[:], scale=1.0,
                 accum_out=row_sum[h, b][:],
             )
 

@@ -2,12 +2,13 @@ import concourse.mybir as mybir
 from concourse.masks import make_identity
 
 F32, BF16, U16 = mybir.dt.float32, mybir.dt.bfloat16, mybir.dt.uint16
-ADD, MULT = mybir.AluOpType.add, mybir.AluOpType.mult
+ADD, MULT, SUBTRACT = mybir.AluOpType.add, mybir.AluOpType.mult, mybir.AluOpType.subtract
 EXP = mybir.ActivationFunctionType.Exp
 FREE_AXIS = mybir.AxisListType.X
 
 P = 128
 HEADS = 4
+LAST = HEADS - 1
 WORDS = 2048
 TOKENS = 512
 BLOCKS = TOKENS // P
@@ -39,12 +40,17 @@ def tile_statementencoder_kernel(tc, word_emb, pos_emb, bo, offs, out):
         bias_rows = held.tile([HEADS, P], F32, name="bias_rows")
         nc.sync.dma_start(bias_rows[:], bo.rearrange("(h d) o -> h (d o)", h=HEADS))
 
-        identity = held.tile([P, P], F32, name="identity")
+        identity = held.tile([P, P], BF16, name="identity")
         make_identity(nc, identity[:])
 
         pooled = held.tile([P, HEADS], F32, name="pooled")
+        nc.gpsimd.memset(pooled[:], 0.0)
 
         x, x_bf16, energy, colsum, expd, row_sum, inv_sum = {}, {}, {}, {}, {}, {}, {}
+        x_t = held.tile([P, TOKENS], BF16, name="x_t")
+        colsum_t = held.tile([P, BLOCKS, HEADS], BF16, name="colsum_t")
+        nc.gpsimd.memset(colsum_t[:], 0.0)
+        parts = []
 
         def embed(h):
             x[h] = held.tile([P, TOKENS], F32, name=f"x{h}")
@@ -82,10 +88,31 @@ def tile_statementencoder_kernel(tc, word_emb, pos_emb, bo, offs, out):
                 start=(b == 0), stop=(b == BLOCKS - 1),
             )
 
+        def transpose_last():
+            x_t_psum = colsums.tile([P, TOKENS], BF16, name="x_t_psum", tag="colsum")
+            for kb in range(BLOCKS):
+                block = slice(kb * P, (kb + 1) * P)
+                nc.tensor.transpose(x_t_psum[:, block], x_bf16[LAST][:, block], identity[:])
+            nc.vector.tensor_copy(x_t[:], x_t_psum[:])
+
+        def add_to_parts(b):
+            if b == 0:
+                parts.append(colsums.tile([P, BLOCKS, BLOCKS], F32, name="parts", tag="colsum"))
+            for kb in range(BLOCKS):
+                nc.tensor.matmul(
+                    parts[0][:, kb, b : b + 1],
+                    expd[LAST, b][:, kb * P : (kb + 1) * P], inv_sum[LAST, b][:, 0:1],
+                    start=True, stop=True,
+                )
+
+        def sum_parts():
+            with nc.allow_low_precision(reason="the column sums are a matmul operand: bfloat16"):
+                nc.vector.reduce_sum(colsum_t[:, :, LAST], parts[0][:], axis=FREE_AXIS)
+
         def pool_head(h):
             weighted = work.tile([P, TOKENS], F32, name="weighted")
             nc.vector.scalar_tensor_tensor(
-                weighted[:], colsum[h][:], 1.0, x[h][:], MULT, MULT, accum_out=pooled[:, h : h + 1]
+                weighted[:], colsum[h][:], X_SCALE, x[h][:], MULT, MULT, accum_out=pooled[:, h : h + 1]
             )
 
         ENERGY_LEAD, INVERT_LAG, COLSUM_LAG = 2, 2, 3
@@ -98,18 +125,35 @@ def tile_statementencoder_kernel(tc, word_emb, pos_emb, bo, offs, out):
                 h, b = pairs[step]
                 if b == 1 and h + 1 < HEADS:
                     embed(h + 1)
+                if (h, b) == (LAST, 0):
+                    transpose_last()
                 exponentials(h, b)
             if 0 <= step - INVERT_LAG < len(pairs):
                 invert(*pairs[step - INVERT_LAG])
             if 0 <= step - COLSUM_LAG < len(pairs):
-                add_to_colsum(*pairs[step - COLSUM_LAG])
-        for h in range(HEADS):
+                h, b = pairs[step - COLSUM_LAG]
+                if h == LAST:
+                    add_to_parts(b)
+                else:
+                    add_to_colsum(h, b)
+        sum_parts()
+        for h in range(LAST):
             pool_head(h)
 
-        pooled_rows = energies.tile([HEADS, P], F32, name="pooled_rows", tag="energy")
-        nc.tensor.transpose(pooled_rows[:], pooled[:], identity[:])
-        out_rows = held.tile([HEADS, P], F32, name="out_rows")
+        rows_psum = energies.tile([HEADS, P], F32, name="rows_psum", tag="energy")
+        high = held.tile([P, HEADS], BF16, name="high")
+        nc.vector.tensor_copy(high[:], pooled[:])
+        low = held.tile([P, HEADS], BF16, name="low")
+        nc.vector.tensor_tensor(low[:], pooled[:], high[:], SUBTRACT)
+        nc.tensor.matmul(rows_psum[:], high[:], identity[:], start=True, stop=False)
+        nc.tensor.matmul(rows_psum[:], low[:], identity[:], start=False, stop=False)
+        for kb in range(BLOCKS):
+            nc.tensor.matmul(
+                rows_psum[:], colsum_t[:, kb, :], x_t[:, kb * P : (kb + 1) * P],
+                start=False, stop=(kb == BLOCKS - 1),
+            )
+        rows = held.tile([HEADS, P], F32, name="rows")
         nc.vector.scalar_tensor_tensor(
-            out_rows[:], pooled_rows[:], 1.0 / TOKENS, bias_rows[:], MULT, ADD
+            rows[:], rows_psum[:], 1.0 / (TOKENS * X_SCALE), bias_rows[:], MULT, ADD
         )
-        nc.sync.dma_start(out.rearrange("(h d) o -> h (d o)", h=HEADS), out_rows[:])
+        nc.sync.dma_start(out.rearrange("(h d) o -> h (d o)", h=HEADS), rows[:])

@@ -21,6 +21,7 @@ def tile_statementencoder_kernel(tc, word_emb, pos_emb, bo, offs, out):
     nc = tc.nc
     with (
         tc.tile_pool(name="held", bufs=1) as held,
+        tc.tile_pool(name="two", bufs=2) as two,
         tc.tile_pool(name="stats", bufs=10) as stats,
         tc.tile_pool(name="work", bufs=6) as work,
         tc.psum_pool(name="energies", bufs=5) as energies,
@@ -33,7 +34,7 @@ def tile_statementencoder_kernel(tc, word_emb, pos_emb, bo, offs, out):
             channels = slice(h * P, (h + 1) * P)
             position = held.tile([P, TOKENS], F32, name=f"position{h}")
             nc.sync.dma_start(position[:], pos_emb[channels, :])
-            word = held.tile([P, WORDS], F32, name=f"word{h}")
+            word = two.tile([P, WORDS], F32, name="word")
             nc.sync.dma_start(word[:], word_emb[channels, :])
             positions.append(position)
             words.append(word)

import concourse.mybir as mybir
from concourse.masks import make_identity

F32, BF16, U16 = mybir.dt.float32, mybir.dt.bfloat16, mybir.dt.uint16
ADD, MULT, SUBTRACT = mybir.AluOpType.add, mybir.AluOpType.mult, mybir.AluOpType.subtract
EXP = mybir.ActivationFunctionType.Exp
FREE_AXIS = mybir.AxisListType.X

P = 128
HEADS = 4
LAST = HEADS - 1
WORDS = 2048
TOKENS = 512
BLOCKS = TOKENS // P
X_SCALE = (HEADS * P) ** -0.25

FLOPS = 2 * HEADS * P * TOKENS * TOKENS + 2 * HEADS * TOKENS * TOKENS + 2 * HEADS * P * TOKENS


def tile_statementencoder_kernel(tc, word_emb, pos_emb, bo, offs, out):
    nc = tc.nc
    with (
        tc.tile_pool(name="held", bufs=1) as held,
        tc.tile_pool(name="two", bufs=2) as two,
        tc.tile_pool(name="stats", bufs=10) as stats,
        tc.tile_pool(name="work", bufs=6) as work,
        tc.psum_pool(name="energies", bufs=5) as energies,
        tc.psum_pool(name="colsums", bufs=3) as colsums,
    ):
        offsets = held.tile([P, TOKENS // 16], U16, name="offsets")
        nc.sync.dma_start(offsets[:], offs)
        words, positions = [], []
        for h in range(HEADS):
            channels = slice(h * P, (h + 1) * P)
            position = held.tile([P, TOKENS], F32, name=f"position{h}")
            nc.sync.dma_start(position[:], pos_emb[channels, :])
            word = two.tile([P, WORDS], F32, name="word")
            nc.sync.dma_start(word[:], word_emb[channels, :])
            positions.append(position)
            words.append(word)
        bias_rows = held.tile([HEADS, P], F32, name="bias_rows")
        nc.sync.dma_start(bias_rows[:], bo.rearrange("(h d) o -> h (d o)", h=HEADS))

        identity = held.tile([P, P], BF16, name="identity")
        make_identity(nc, identity[:])

        pooled = held.tile([P, HEADS], F32, name="pooled")
        nc.gpsimd.memset(pooled[:], 0.0)

        x, x_bf16, energy, colsum, expd, row_sum, inv_sum = {}, {}, {}, {}, {}, {}, {}
        x_t = held.tile([P, TOKENS], BF16, name="x_t")
        colsum_t = held.tile([P, BLOCKS, HEADS], BF16, name="colsum_t")
        nc.gpsimd.memset(colsum_t[:], 0.0)
        parts = []

        def embed(h):
            x[h] = held.tile([P, TOKENS], F32, name=f"x{h}")
            nc.vector.tensor_tensor(x[h][:], words[h][:].indirect(offsets[:]), positions[h][:], ADD)
            x_bf16[h] = held.tile([P, TOKENS], BF16, name=f"x_bf16_{h}")
            nc.gpsimd.tensor_scalar(x_bf16[h][:], x[h][:], X_SCALE, 0.0, MULT, ADD)

        def energies_of(h, b):
            energy[h, b] = energies.tile([P, TOKENS], F32, name="energy")
            nc.tensor.matmul(
                energy[h, b][:], x_bf16[h][:, b * P : (b + 1) * P], x_bf16[h][:],
                start=True, stop=True,
            )

        def exponentials(h, b):
            neg_max = stats.tile([P, 1], F32, name="neg_max")
            nc.vector.reduce_max(neg_max[:], energy[h, b][:], axis=FREE_AXIS, negate=True)
            expd[h, b] = work.tile([P, TOKENS], BF16, name="expd")
            row_sum[h, b] = stats.tile([P, 1], F32, name="row_sum")
            nc.scalar.activation(
                expd[h, b][:], energy[h, b][:], EXP, bias=neg_max[:], scale=1.0,
                accum_out=row_sum[h, b][:],
            )

        def invert(h, b):
            inv_sum[h, b] = stats.tile([P, 1], BF16, name="inv_sum")
            with nc.allow_low_precision(reason="1 / sum is a matmul operand: bfloat16"):
                nc.vector.reciprocal(inv_sum[h, b][:], row_sum[h, b][:])

        def add_to_colsum(h, b):
            if b == 0:
                colsum[h] = colsums.tile([P, TOKENS], F32, name="colsum")
            nc.tensor.matmul(
                colsum[h][:], inv_sum[h, b][:, 0:1].to_broadcast([P, P]), expd[h, b][:],
                start=(b == 0), stop=(b == BLOCKS - 1),
            )

        def transpose_last():
            x_t_psum = colsums.tile([P, TOKENS], BF16, name="x_t_psum", tag="colsum")
            for kb in range(BLOCKS):
                block = slice(kb * P, (kb + 1) * P)
                nc.tensor.transpose(x_t_psum[:, block], x_bf16[LAST][:, block], identity[:])
            nc.vector.tensor_copy(x_t[:], x_t_psum[:])

        def add_to_parts(b):
            if b == 0:
                parts.append(colsums.tile([P, BLOCKS, BLOCKS], F32, name="parts", tag="colsum"))
            for kb in range(BLOCKS):
                nc.tensor.matmul(
                    parts[0][:, kb, b : b + 1],
                    expd[LAST, b][:, kb * P : (kb + 1) * P], inv_sum[LAST, b][:, 0:1],
                    start=True, stop=True,
                )

        def sum_parts():
            with nc.allow_low_precision(reason="the column sums are a matmul operand: bfloat16"):
                nc.vector.reduce_sum(colsum_t[:, :, LAST], parts[0][:], axis=FREE_AXIS)

        def pool_head(h):
            weighted = work.tile([P, TOKENS], F32, name="weighted")
            nc.vector.scalar_tensor_tensor(
                weighted[:], colsum[h][:], X_SCALE, x[h][:], MULT, MULT, accum_out=pooled[:, h : h + 1]
            )

        ENERGY_LEAD, INVERT_LAG, COLSUM_LAG = 2, 2, 3
        pairs = [(h, b) for h in range(HEADS) for b in range(BLOCKS)]
        embed(0)
        for step in range(-ENERGY_LEAD, len(pairs) + COLSUM_LAG):
            if step + ENERGY_LEAD < len(pairs):
                energies_of(*pairs[step + ENERGY_LEAD])
            if 0 <= step < len(pairs):
                h, b = pairs[step]
                if b == 1 and h + 1 < HEADS:
                    embed(h + 1)
                if (h, b) == (LAST, 0):
                    transpose_last()
                exponentials(h, b)
            if 0 <= step - INVERT_LAG < len(pairs):
                invert(*pairs[step - INVERT_LAG])
            if 0 <= step - COLSUM_LAG < len(pairs):
                h, b = pairs[step - COLSUM_LAG]
                if h == LAST:
                    add_to_parts(b)
                else:
                    add_to_colsum(h, b)
        sum_parts()
        for h in range(LAST):
            pool_head(h)

        rows_psum = energies.tile([HEADS, P], F32, name="rows_psum", tag="energy")
        high = held.tile([P, HEADS], BF16, name="high")
        nc.vector.tensor_copy(high[:], pooled[:])
        low = held.tile([P, HEADS], BF16, name="low")
        nc.vector.tensor_tensor(low[:], pooled[:], high[:], SUBTRACT)
        nc.tensor.matmul(rows_psum[:], high[:], identity[:], start=True, stop=False)
        nc.tensor.matmul(rows_psum[:], low[:], identity[:], start=False, stop=False)
        for kb in range(BLOCKS):
            nc.tensor.matmul(
                rows_psum[:], colsum_t[:, kb, :], x_t[:, kb * P : (kb + 1) * P],
                start=False, stop=(kb == BLOCKS - 1),
            )
        rows = held.tile([HEADS, P], F32, name="rows")
        nc.vector.scalar_tensor_tensor(
            rows[:], rows_psum[:], 1.0 / (TOKENS * X_SCALE), bias_rows[:], MULT, ADD
        )
        nc.sync.dma_start(out.rearrange("(h d) o -> h (d o)", h=HEADS), rows[:])
